import numpy as np
import ml_dtypes


def mxq(x, axis, fmt="e4m3"):
    dtype, down = {"e4m3": (ml_dtypes.float8_e4m3fn, 7), "e5m2": (ml_dtypes.float8_e5m2, 14)}[fmt]
    v = np.moveaxis(np.asarray(x, np.float32).astype(ml_dtypes.bfloat16).astype(np.float64), axis, -1)
    blocks = v.reshape(v.shape[:-1] + (-1, 32))
    amax = np.abs(blocks).max(-1, keepdims=True)
    byte = np.maximum(np.where(amax > 0, np.frexp(amax)[1] - 1 + 127, 0) - down, 1)
    scale = np.exp2(byte - 127.0)
    codes = (blocks / scale).astype(np.float32).astype(dtype).astype(np.float64)
    return np.moveaxis((codes * scale).reshape(v.shape), -1, axis)


WIDE = False


def mx_kscale(k):
    if not WIDE:
        return np.ones(k)
    levels = np.array([10, -10, 5, -5, 0])
    a = np.random.permutation(np.resize(levels, k // 512 * 4)).reshape(k // 512, 4)
    idx = np.arange(k)
    return np.exp2(a[idx // 512, idx % 128 // 32])


BF16 = ml_dtypes.bfloat16


def bf(x):
    return np.asarray(x, np.float32).astype(BF16)


def f64(x):
    return np.asarray(x).astype(np.float64)


E2M1 = np.array([0.0, 0.5, 1.0, 1.5, 2.0, 3.0, 4.0, 6.0, -0.0, -0.5, -1.0, -1.5, -2.0, -3.0, -4.0, -6.0])


def pack_weight(w, fmt):
    k, n = w.shape
    w = f64(bf(w)).reshape(k // 32, 32, n)
    amax = np.abs(w).max(1)
    if fmt == "e4m3":
        byte = np.frexp(amax)[1] - 1 + 127 - 7
    else:
        mant, ex = np.frexp(amax / 6.0)
        byte = np.where(mant > 0.5, ex, ex - 1) + 127
    byte = np.clip(np.where(amax > 0, byte, 1), 1, 254)
    scaled = (w * np.exp2(127.0 - byte)[:, None, :]).reshape(k, n).astype(np.float32)
    by_word = np.ascontiguousarray(scaled.reshape(k // 512, 128, 4, n).transpose(0, 1, 3, 2))
    if fmt == "e4m3":
        words = by_word.astype(ml_dtypes.float8_e4m3fn).view(np.uint8)
    else:
        c = by_word.astype(ml_dtypes.float4_e2m1fn).view(np.uint8) & 0xF
        words = c[..., 0::2] | (c[..., 1::2] << 4)
    return np.ascontiguousarray(words), np.ascontiguousarray(byte.astype(np.uint8).reshape(k // 512, 16, n))


def unpack_weight(words, scales, fmt):
    g, p, n, _ = words.shape
    if fmt == "e4m3":
        vals = np.ascontiguousarray(words).view(ml_dtypes.float8_e4m3fn).astype(np.float64)
    else:
        nib = np.empty((g, p, n, 4), np.uint8)
        nib[..., 0::2] = words & 0xF
        nib[..., 1::2] = words >> 4
        vals = E2M1[nib]
    vals = vals * np.repeat(np.exp2(scales.astype(np.float64) - 127.0), 8, axis=1)[..., None]
    return vals.transpose(0, 1, 3, 2).reshape(g * 512, n)


B, P, D, DFF = 2, 64, 8192, 512


def sigmoid(v):
    return 1.0 / (1.0 + np.exp(-v))


def setup_inputs():
    s = mx_kscale(D)
    inp = {
        'Zi': bf(np.random.standard_normal((B, P, D)) * s),
        'Ci': bf(np.random.standard_normal((B, P, DFF))),
        'Mi': bf(np.random.standard_normal((B, P, DFF))),
        'Hi': bf(np.random.standard_normal((B, P, DFF))),
        'Ni': bf(np.random.uniform(0.5, 1.5, (B, P, DFF))),
        'm': bf(np.random.uniform(0.0, 1.0, (B, P, 1))),
    }
    for n in ('WI', 'WF', 'WO', 'WZ'):
        words, scales = pack_weight(np.random.standard_normal((DFF, DFF)) * 0.7 / np.sqrt(DFF), 'e4m3')
        inp[n + '_w_words'] = words
        inp[n + '_w_scales'] = scales
        inp[n + '_b'] = bf(np.random.standard_normal(DFF) * 0.3)
    for n in ('RI', 'RF', 'RO', 'RZ'):
        words, scales = pack_weight(np.random.standard_normal((D, DFF)) * 0.7 / np.sqrt(D) / s[:, None], 'e4m3')
        inp[n + '_w_words'] = words
        inp[n + '_w_scales'] = scales
        inp[n + '_b'] = bf(np.random.standard_normal(DFF) * 0.3)
    return inp


def reference(Zi, Ci, Mi, Hi, Ni, m,
              WI_w_words, WI_w_scales, WI_b, WF_w_words, WF_w_scales, WF_b,
              WO_w_words, WO_w_scales, WO_b, WZ_w_words, WZ_w_scales, WZ_b,
              RI_w_words, RI_w_scales, RI_b, RF_w_words, RF_w_scales, RF_b,
              RO_w_words, RO_w_scales, RO_b, RZ_w_words, RZ_w_scales, RZ_b):
    Zi, Ci, Mi, Hi, Ni, m = f64(Zi), f64(Ci), f64(Mi), f64(Hi), f64(Ni), f64(m)
    Wh = np.concatenate([unpack_weight(WI_w_words, WI_w_scales, 'e4m3'), unpack_weight(WF_w_words, WF_w_scales, 'e4m3'),
                         unpack_weight(WO_w_words, WO_w_scales, 'e4m3'), unpack_weight(WZ_w_words, WZ_w_scales, 'e4m3')], axis=1)
    Wz = np.concatenate([unpack_weight(RI_w_words, RI_w_scales, 'e4m3'), unpack_weight(RF_w_words, RF_w_scales, 'e4m3'),
                         unpack_weight(RO_w_words, RO_w_scales, 'e4m3'), unpack_weight(RZ_w_words, RZ_w_scales, 'e4m3')], axis=1)
    bias = np.concatenate([f64(WI_b) + f64(RI_b), f64(WF_b) + f64(RF_b), f64(WO_b) + f64(RO_b), f64(WZ_b) + f64(RZ_b)])
    gates = (mxq(Hi, 2, 'e4m3') @ Wh) + (mxq(Zi, 2, 'e4m3') @ Wz) + bias
    I_tilde, F_tilde, O_tilde, Z_tilde = np.split(gates, 4, axis=-1)

    M_t = np.maximum(F_tilde + Mi, I_tilde)
    I_t = np.exp(I_tilde - M_t)
    F_t = np.exp(F_tilde + Mi - M_t)
    O_t = sigmoid(O_tilde)
    N_t = F_t * Ni + I_t
    Z_t = np.tanh(Z_tilde)
    C_t = (Ci * F_t + Z_t * I_t) * m + (1.0 - m) * Ci
    H_t = O_t * (C_t / N_t) * m + (1.0 - m) * Hi
    return (C_t, M_t, H_t, N_t)

@@ -1,0 +1,260 @@
+from contextlib import ExitStack
+
+import concourse.mybir as mybir
+from concourse.masks import make_identity
+
+BF16 = mybir.dt.bfloat16
+F32 = mybir.dt.float32
+I32 = mybir.dt.int32
+U8 = mybir.dt.uint8
+U32 = mybir.dt.uint32
+FP8X4 = mybir.dt.float8_e4m3fn_x4
+ALU = mybir.AluOpType
+ACT = mybir.ActivationFunctionType
+
+P = 128
+PACK = 4
+K_PASS = P * PACK
+D = 8192
+DFF = 512
+Z_GROUPS = D // K_PASS
+HI_GROUP = Z_GROUPS
+CHUNK = 4
+PAIR = 2
+QUADRANTS = 4
+LIVE = 4
+
+GATE_ORDER = ("I", "F", "Z", "O")
+
+FLOPS = 2 * P * (D + DFF) * 4 * DFF
+
+
+def tile_customlstmcell_k_kernel(
+    tc, Zi, Ci, Mi, Hi, Ni, m,
+    WI_w_words, WI_w_scales, WI_b, WF_w_words, WF_w_scales, WF_b,
+    WO_w_words, WO_w_scales, WO_b, WZ_w_words, WZ_w_scales, WZ_b,
+    RI_w_words, RI_w_scales, RI_b, RF_w_words, RF_w_scales, RF_b,
+    RO_w_words, RO_w_scales, RO_b, RZ_w_words, RZ_w_scales, RZ_b,
+    out_0, out_1, out_2, out_3,
+):
+    nc = tc.nc
+    w_in = {
+        "I": (WI_w_words, WI_w_scales, WI_b),
+        "F": (WF_w_words, WF_w_scales, WF_b),
+        "O": (WO_w_words, WO_w_scales, WO_b),
+        "Z": (WZ_w_words, WZ_w_scales, WZ_b),
+    }
+    r_in = {
+        "I": (RI_w_words, RI_w_scales, RI_b),
+        "F": (RF_w_words, RF_w_scales, RF_b),
+        "O": (RO_w_words, RO_w_scales, RO_b),
+        "Z": (RZ_w_words, RZ_w_scales, RZ_b),
+    }
+    plane_start = {gate: LIVE * i for i, gate in enumerate(GATE_ORDER)}
+    bias_cols = {gate: slice(DFF * i, DFF * (i + 1)) for i, gate in enumerate(GATE_ORDER)}
+
+    with ExitStack() as ctx:
+        keep = ctx.enter_context(tc.tile_pool(name="keep", bufs=1))
+        stage = ctx.enter_context(tc.tile_pool(name="stage", bufs=2))
+        acc_pool = ctx.enter_context(tc.psum_pool(name="acc", bufs=1))
+        spare = ctx.enter_context(tc.psum_pool(name="spare", bufs=4))
+
+        r_planes = keep.tile([P, Z_GROUPS, DFF], U8, align_bytes=64)
+        w_planes = keep.tile([P, DFF], U8, align_bytes=64)
+        nc.vector.memset(r_planes[:].bitcast(I32), 0)
+        nc.vector.memset(w_planes[:].bitcast(I32), 0)
+        bias_rows = keep.tile([P, 4 * DFF], BF16)
+        nc.vector.memset(bias_rows[:], 0.0)
+        ones = keep.tile([P, P], BF16)
+        nc.vector.memset(ones[:], 1.0)
+        ident = keep.tile([P, P], F32)
+        make_identity(nc, ident[:])
+
+        for gate in GATE_ORDER:
+            first = plane_start[gate]
+            for quad in range(QUADRANTS):
+                rows = slice(32 * quad + first, 32 * quad + first + LIVE)
+                nc.gpsimd.dma_start(
+                    out=r_planes[rows, :, :].bitcast(F32),
+                    in_=r_in[gate][1][:, LIVE * quad : LIVE * (quad + 1), :].rearrange("g r n -> r g n").bitcast(F32),
+                )
+        for gate in GATE_ORDER:
+            first = plane_start[gate]
+            for quad in range(QUADRANTS):
+                rows = slice(32 * quad + first, 32 * quad + first + LIVE)
+                nc.gpsimd.dma_start(
+                    out=w_planes[rows, :].bitcast(F32),
+                    in_=w_in[gate][1][0, LIVE * quad : LIVE * (quad + 1), :].bitcast(F32),
+                )
+
+        zi_rows = Zi.flatten_outer_dims()
+        zi_sb = [keep.tile([P, CHUNK * K_PASS], BF16, name="zi_sb%d" % c) for c in range(Z_GROUPS // CHUNK)]
+        hi_sb = keep.tile([P, DFF], BF16)
+        ci_sb = keep.tile([P, DFF], BF16)
+        mi_sb = keep.tile([P, DFF], BF16)
+        ni_sb = keep.tile([P, DFF], BF16)
+        m_sb = keep.tile([P, 1], BF16)
+        r_words = {
+            gate: [
+                keep.tile([P, CHUNK, PACK * DFF], U8, name="r_words_%s%d" % (gate, c), align_bytes=64)
+                for c in range(Z_GROUPS // CHUNK)
+            ]
+            for gate in GATE_ORDER
+        }
+        w_words = {
+            gate: keep.tile([P, PACK * DFF], U8, name="w_words_%s" % gate, align_bytes=64) for gate in GATE_ORDER
+        }
+
+        big_loads = []
+        for c, zi_chunk in enumerate(zi_sb):
+            big_loads.append((zi_chunk[:], zi_rows[:, CHUNK * K_PASS * c : CHUNK * K_PASS * (c + 1)]))
+        big_loads.append((hi_sb[:], Hi.flatten_outer_dims()))
+        for gate in GATE_ORDER:
+            by_partition = r_in[gate][0].rearrange("g p n t -> p g (n t)")
+            for c, chunk in enumerate(r_words[gate]):
+                big_loads.append((chunk[:].bitcast(I32), by_partition[:, CHUNK * c : CHUNK * (c + 1), :].bitcast(I32)))
+            big_loads.append((w_words[gate][:].bitcast(I32), w_in[gate][0][0].rearrange("p n t -> p (n t)").bitcast(I32)))
+
+        small_loads = []
+        for gate in GATE_ORDER:
+            small_loads.append((bias_rows[0:1, bias_cols[gate]], w_in[gate][2].unsqueeze(0)))
+            small_loads.append((bias_rows[1:2, bias_cols[gate]], r_in[gate][2].unsqueeze(0)))
+        small_loads.append((mi_sb[:], Mi.flatten_outer_dims()))
+        small_loads.append((m_sb[:], m.flatten_outer_dims()))
+        small_loads.append((ci_sb[:], Ci.flatten_outer_dims()))
+        small_loads.append((ni_sb[:], Ni.flatten_outer_dims()))
+
+        for i, (dst, src) in enumerate(big_loads):
+            nc.sync.dma_start(out=dst, in_=src)
+            if i < len(small_loads):
+                nc.sync.dma_start(out=small_loads[i][0], in_=small_loads[i][1])
+
+        x_codes = keep.tile([P, Z_GROUPS + 1, P], U32, align_bytes=64)
+        x_scales = keep.tile([P, Z_GROUPS + 1, P], U8, align_bytes=64)
+
+        def quantise(x_sb, n_groups, first_group, bank_parity):
+            words = x_sb[:].bitcast(F32)
+            grouped = stage.tile([P, n_groups * K_PASS], BF16, tag="grouped", align_bytes=64)
+            grouped_words = grouped[:].bitcast(F32).rearrange("p (g r u) -> p g r u", g=n_groups, u=PAIR)
+            in_bank = min(2, n_groups)
+            for b in range(n_groups // in_bank):
+                bank = spare.tile([P, in_bank, PAIR, P], F32, tag="spare")
+                for j in range(in_bank):
+                    g = in_bank * b + j
+                    for u in range(PAIR):
+                        nc.tensor.transpose(
+                            bank[:, j, u, :], words[:, 256 * g + u : 256 * (g + 1) : PAIR], ident[:]
+                        )
+                dst = grouped_words[:, in_bank * b : in_bank * (b + 1)]
+                src = bank[:].rearrange("p g u r -> p g r u")
+                if (b + bank_parity) % 2 == 0:
+                    nc.vector.tensor_copy(out=dst, in_=src)
+                else:
+                    nc.scalar.copy(out=dst, in_=src)
+            groups = slice(first_group, first_group + n_groups)
+            nc.vector.quantize_mx(
+                out=x_codes[:, groups, :].rearrange("p g r -> p (g r)").bitcast(FP8X4),
+                scales=x_scales[:, groups, :].rearrange("p g r -> p (g r)"),
+                in_=grouped[:],
+            )
+
+        for c, zi_chunk in enumerate(zi_sb):
+            quantise(zi_chunk, CHUNK, CHUNK * c, 0)
+        quantise(hi_sb, 1, HI_GROUP, 0)
+
+        def gate_products(gate):
+            acc = acc_pool.tile([P, DFF], F32, name="acc_%s" % gate)
+            first = plane_start[gate]
+            for g in range(Z_GROUPS):
+                nc.tensor.matmul_mx(
+                    out=acc[:],
+                    lhsT=x_codes[:, g, :].bitcast(FP8X4),
+                    lhsT_scale=x_scales[:, g, :],
+                    rhs=r_words[gate][g // CHUNK][:, g % CHUNK, :].bitcast(FP8X4),
+                    rhs_scale=r_planes[first:P, g, :],
+                    start=(g == 0),
+                    stop=False,
+                )
+            nc.tensor.matmul_mx(
+                out=acc[:],
+                lhsT=x_codes[:, HI_GROUP, :].bitcast(FP8X4),
+                lhsT_scale=x_scales[:, HI_GROUP, :],
+                rhs=w_words[gate][:].bitcast(FP8X4),
+                rhs_scale=w_planes[first:P, :],
+                start=False,
+                stop=True,
+            )
+            return acc
+
+        def f32_tile(name):
+            return keep.tile([P, DFF], F32, name=name)
+
+        acc_i = gate_products("I")
+
+        pre = {}
+        for gate in GATE_ORDER:
+            bias_bank = spare.tile([P, DFF], F32, tag="spare")
+            nc.tensor.matmul(out=bias_bank[:], lhsT=ones[:], rhs=bias_rows[:, bias_cols[gate]], start=True, stop=True)
+            pre[gate] = f32_tile("pre_%s" % gate)
+            if gate == "F":
+                nc.vector.tensor_add(out=pre[gate][:], in0=bias_bank[:], in1=mi_sb[:])
+            else:
+                nc.scalar.copy(out=pre[gate][:], in_=bias_bank[:])
+        m_f32 = keep.tile([P, 1], F32)
+        nc.vector.tensor_copy(out=m_f32[:], in_=m_sb[:])
+        one_minus_m = keep.tile([P, 1], F32)
+        nc.vector.tensor_scalar(out=one_minus_m[:], in0=m_f32[:], scalar1=-1.0, scalar2=1.0, op0=ALU.mult, op1=ALU.add)
+        half_m = keep.tile([P, 1], F32)
+        nc.vector.tensor_scalar_mul(out=half_m[:], in0=m_f32[:], scalar1=0.5)
+        ci_m = f32_tile("ci_m")
+        nc.vector.tensor_scalar_mul(out=ci_m[:], in0=ci_sb[:], scalar1=m_f32[:, 0:1])
+        ci_keep = f32_tile("ci_keep")
+        nc.vector.tensor_scalar_mul(out=ci_keep[:], in0=ci_sb[:], scalar1=one_minus_m[:, 0:1])
+        h_rest = f32_tile("h_rest")
+        nc.vector.tensor_scalar_mul(out=h_rest[:], in0=hi_sb[:], scalar1=one_minus_m[:, 0:1])
+
+        acc_f = gate_products("F")
+
+        nc.vector.tensor_add(out=pre["I"][:], in0=acc_i[:], in1=pre["I"][:])
+        nc.vector.tensor_add(out=pre["F"][:], in0=acc_f[:], in1=pre["F"][:])
+        m_t = f32_tile("m_t")
+        nc.vector.tensor_max(out=m_t[:], in0=pre["F"][:], in1=pre["I"][:])
+        nc.sync.dma_start(out=out_1.flatten_outer_dims(), in_=m_t[:])
+        i_t = f32_tile("i_t")
+        nc.vector.tensor_sub(out=i_t[:], in0=pre["I"][:], in1=m_t[:])
+        nc.scalar.activation(out=i_t[:], in_=i_t[:], func=ACT.Exp)
+        f_t = f32_tile("f_t")
+        nc.vector.tensor_sub(out=f_t[:], in0=pre["F"][:], in1=m_t[:])
+        nc.scalar.activation(out=f_t[:], in_=f_t[:], func=ACT.Exp)
+        n_t = f32_tile("n_t")
+        nc.vector.tensor_mul(out=n_t[:], in0=f_t[:], in1=ni_sb[:])
+        nc.vector.tensor_add(out=n_t[:], in0=n_t[:], in1=i_t[:])
+        nc.sync.dma_start(out=out_3.flatten_outer_dims(), in_=n_t[:])
+        one_over_n = f32_tile("one_over_n")
+        nc.vector.reciprocal(out=one_over_n[:], in_=n_t[:])
+        c_t = f32_tile("c_t")
+        nc.vector.tensor_mul(out=c_t[:], in0=f_t[:], in1=ci_m[:])
+        nc.vector.tensor_add(out=c_t[:], in0=c_t[:], in1=ci_keep[:])
+
+        acc_z = gate_products("Z")
+
+        nc.vector.tensor_add(out=pre["Z"][:], in0=acc_z[:], in1=pre["Z"][:])
+        nc.scalar.activation(out=pre["Z"][:], in_=pre["Z"][:], func=ACT.Tanh)
+        nc.vector.tensor_mul(out=pre["Z"][:], in0=pre["Z"][:], in1=i_t[:])
+        nc.vector.scalar_tensor_tensor(
+            out=c_t[:], in0=pre["Z"][:], scalar=m_f32[:, 0:1], in1=c_t[:], op0=ALU.mult, op1=ALU.add
+        )
+        nc.sync.dma_start(out=out_0.flatten_outer_dims(), in_=c_t[:])
+        h_gain = f32_tile("h_gain")
+        nc.vector.scalar_tensor_tensor(
+            out=h_gain[:], in0=c_t[:], scalar=half_m[:, 0:1], in1=one_over_n[:], op0=ALU.mult, op1=ALU.mult
+        )
+        nc.vector.tensor_add(out=h_rest[:], in0=h_rest[:], in1=h_gain[:])
+
+        acc_o = gate_products("O")
+
+        nc.vector.tensor_add(out=pre["O"][:], in0=acc_o[:], in1=pre["O"][:])
+        nc.scalar.activation(out=pre["O"][:], in_=pre["O"][:], func=ACT.Tanh, scale=0.5)
+        nc.vector.tensor_mul(out=pre["O"][:], in0=pre["O"][:], in1=h_gain[:])
+        nc.vector.tensor_add(out=pre["O"][:], in0=pre["O"][:], in1=h_rest[:])
+        nc.sync.dma_start(out=out_2.flatten_outer_dims(), in_=pre["O"][:])

@@ -20,9 +20,11 @@ DFF = 512
 Z_GROUPS = D // K_PASS
 HI_GROUP = Z_GROUPS
 CHUNK = 4
+N_CHUNKS = Z_GROUPS // CHUNK
 PAIR = 2
 QUADRANTS = 4
 LIVE = 4
+SMALL_PER_BIG = 2
 
 GATE_ORDER = ("I", "F", "Z", "O")
 
@@ -53,114 +55,133 @@ def tile_customlstmcell_k_kernel(
     plane_start = {gate: LIVE * i for i, gate in enumerate(GATE_ORDER)}
     bias_cols = {gate: slice(DFF * i, DFF * (i + 1)) for i, gate in enumerate(GATE_ORDER)}
 
+    def live_rows(gate, quad):
+        return slice(32 * quad + plane_start[gate], 32 * quad + plane_start[gate] + LIVE)
+
     with ExitStack() as ctx:
         keep = ctx.enter_context(tc.tile_pool(name="keep", bufs=1))
-        stage = ctx.enter_context(tc.tile_pool(name="stage", bufs=2))
         acc_pool = ctx.enter_context(tc.psum_pool(name="acc", bufs=1))
         spare = ctx.enter_context(tc.psum_pool(name="spare", bufs=4))
 
-        r_planes = keep.tile([P, Z_GROUPS, DFF], U8, align_bytes=64)
-        w_planes = keep.tile([P, DFF], U8, align_bytes=64)
-        nc.vector.memset(r_planes[:].bitcast(I32), 0)
-        nc.vector.memset(w_planes[:].bitcast(I32), 0)
+        r_planes = {
+            gate: keep.tile([P, Z_GROUPS, DFF], U8, name="r_planes_%s" % gate, align_bytes=64) for gate in GATE_ORDER
+        }
+        w_planes = {gate: keep.tile([P, DFF], U8, name="w_planes_%s" % gate, align_bytes=64) for gate in GATE_ORDER}
         bias_rows = keep.tile([P, 4 * DFF], BF16)
-        nc.vector.memset(bias_rows[:], 0.0)
         ones = keep.tile([P, P], BF16)
-        nc.vector.memset(ones[:], 1.0)
         ident = keep.tile([P, P], F32)
+        for gate in GATE_ORDER:
+            nc.vector.memset(w_planes[gate][:].bitcast(I32), 0)
+        nc.vector.memset(r_planes[GATE_ORDER[0]][:].bitcast(I32), 0)
+        nc.vector.memset(bias_rows[:], 0.0)
+        nc.vector.memset(ones[:], 1.0)
+        for gate in GATE_ORDER[1:]:
+            nc.vector.memset(r_planes[gate][:].bitcast(I32), 0)
         make_identity(nc, ident[:])
 
-        for gate in GATE_ORDER:
-            first = plane_start[gate]
-            for quad in range(QUADRANTS):
-                rows = slice(32 * quad + first, 32 * quad + first + LIVE)
-                nc.gpsimd.dma_start(
-                    out=r_planes[rows, :, :].bitcast(F32),
-                    in_=r_in[gate][1][:, LIVE * quad : LIVE * (quad + 1), :].rearrange("g r n -> r g n").bitcast(F32),
-                )
-        for gate in GATE_ORDER:
-            first = plane_start[gate]
-            for quad in range(QUADRANTS):
-                rows = slice(32 * quad + first, 32 * quad + first + LIVE)
-                nc.gpsimd.dma_start(
-                    out=w_planes[rows, :].bitcast(F32),
-                    in_=w_in[gate][1][0, LIVE * quad : LIVE * (quad + 1), :].bitcast(F32),
-                )
-
-        zi_rows = Zi.flatten_outer_dims()
-        zi_sb = [keep.tile([P, CHUNK * K_PASS], BF16, name="zi_sb%d" % c) for c in range(Z_GROUPS // CHUNK)]
-        hi_sb = keep.tile([P, DFF], BF16)
-        ci_sb = keep.tile([P, DFF], BF16)
-        mi_sb = keep.tile([P, DFF], BF16)
-        ni_sb = keep.tile([P, DFF], BF16)
-        m_sb = keep.tile([P, 1], BF16)
         r_words = {
             gate: [
                 keep.tile([P, CHUNK, PACK * DFF], U8, name="r_words_%s%d" % (gate, c), align_bytes=64)
-                for c in range(Z_GROUPS // CHUNK)
+                for c in range(N_CHUNKS)
             ]
             for gate in GATE_ORDER
         }
         w_words = {
             gate: keep.tile([P, PACK * DFF], U8, name="w_words_%s" % gate, align_bytes=64) for gate in GATE_ORDER
         }
-
-        big_loads = []
-        for c, zi_chunk in enumerate(zi_sb):
-            big_loads.append((zi_chunk[:], zi_rows[:, CHUNK * K_PASS * c : CHUNK * K_PASS * (c + 1)]))
-        big_loads.append((hi_sb[:], Hi.flatten_outer_dims()))
-        for gate in GATE_ORDER:
-            by_partition = r_in[gate][0].rearrange("g p n t -> p g (n t)")
-            for c, chunk in enumerate(r_words[gate]):
-                big_loads.append((chunk[:].bitcast(I32), by_partition[:, CHUNK * c : CHUNK * (c + 1), :].bitcast(I32)))
-            big_loads.append((w_words[gate][:].bitcast(I32), w_in[gate][0][0].rearrange("p n t -> p (n t)").bitcast(I32)))
-
-        small_loads = []
-        for gate in GATE_ORDER:
-            small_loads.append((bias_rows[0:1, bias_cols[gate]], w_in[gate][2].unsqueeze(0)))
-            small_loads.append((bias_rows[1:2, bias_cols[gate]], r_in[gate][2].unsqueeze(0)))
-        small_loads.append((mi_sb[:], Mi.flatten_outer_dims()))
-        small_loads.append((m_sb[:], m.flatten_outer_dims()))
-        small_loads.append((ci_sb[:], Ci.flatten_outer_dims()))
-        small_loads.append((ni_sb[:], Ni.flatten_outer_dims()))
-
-        for i, (dst, src) in enumerate(big_loads):
-            nc.sync.dma_start(out=dst, in_=src)
-            if i < len(small_loads):
-                nc.sync.dma_start(out=small_loads[i][0], in_=small_loads[i][1])
-
+        hi_sb = keep.tile([P, DFF], BF16)
+        ci_sb = keep.tile([P, DFF], BF16)
+        mi_sb = keep.tile([P, DFF], BF16)
+        ni_sb = keep.tile([P, DFF], BF16)
+        m_sb = keep.tile([P, 1], BF16)
         x_codes = keep.tile([P, Z_GROUPS + 1, P], U32, align_bytes=64)
         x_scales = keep.tile([P, Z_GROUPS + 1, P], U8, align_bytes=64)
 
-        def quantise(x_sb, n_groups, first_group, bank_parity):
-            words = x_sb[:].bitcast(F32)
-            grouped = stage.tile([P, n_groups * K_PASS], BF16, tag="grouped", align_bytes=64)
-            grouped_words = grouped[:].bitcast(F32).rearrange("p (g r u) -> p g r u", g=n_groups, u=PAIR)
-            in_bank = min(2, n_groups)
-            for b in range(n_groups // in_bank):
-                bank = spare.tile([P, in_bank, PAIR, P], F32, tag="spare")
-                for j in range(in_bank):
-                    g = in_bank * b + j
-                    for u in range(PAIR):
-                        nc.tensor.transpose(
-                            bank[:, j, u, :], words[:, 256 * g + u : 256 * (g + 1) : PAIR], ident[:]
-                        )
-                dst = grouped_words[:, in_bank * b : in_bank * (b + 1)]
-                src = bank[:].rearrange("p g u r -> p g r u")
-                if (b + bank_parity) % 2 == 0:
-                    nc.vector.tensor_copy(out=dst, in_=src)
-                else:
-                    nc.scalar.copy(out=dst, in_=src)
-            groups = slice(first_group, first_group + n_groups)
-            nc.vector.quantize_mx(
-                out=x_codes[:, groups, :].rearrange("p g r -> p (g r)").bitcast(FP8X4),
-                scales=x_scales[:, groups, :].rearrange("p g r -> p (g r)"),
-                in_=grouped[:],
-            )
+        for gate in GATE_ORDER:
+            for quad in range(QUADRANTS):
+                nc.gpsimd.dma_start(
+                    out=r_planes[gate][live_rows(gate, quad), :, :].bitcast(F32),
+                    in_=r_in[gate][1][:, LIVE * quad : LIVE * (quad + 1), :].rearrange("g r n -> r g n").bitcast(F32),
+                )
 
-        for c, zi_chunk in enumerate(zi_sb):
-            quantise(zi_chunk, CHUNK, CHUNK * c, 0)
-        quantise(hi_sb, 1, HI_GROUP, 0)
+        def w_scale_loads(gate):
+            return [
+                (
+                    w_planes[gate][live_rows(gate, quad), :].bitcast(I32),
+                    w_in[gate][1][0, LIVE * quad : LIVE * (quad + 1), :].bitcast(I32),
+                )
+                for quad in range(QUADRANTS)
+            ]
+
+        with tc.tile_pool(name="x_rows", bufs=1) as x_rows, tc.tile_pool(name="stage", bufs=2) as stage:
+            zi_rows = Zi.flatten_outer_dims()
+            zi_sb = [x_rows.tile([P, CHUNK * K_PASS], BF16, name="zi_sb%d" % c) for c in range(N_CHUNKS)]
+            big_loads = []
+            for c, zi_chunk in enumerate(zi_sb):
+                big_loads.append((zi_chunk[:], zi_rows[:, CHUNK * K_PASS * c : CHUNK * K_PASS * (c + 1)]))
+            big_loads.append((hi_sb[:], Hi.flatten_outer_dims()))
+            for gate in GATE_ORDER:
+                by_partition = r_in[gate][0].rearrange("g p n t -> p g (n t)")
+                for c, chunk in enumerate(r_words[gate]):
+                    big_loads.append(
+                        (chunk[:].bitcast(I32), by_partition[:, CHUNK * c : CHUNK * (c + 1), :].bitcast(I32))
+                    )
+                big_loads.append(
+                    (w_words[gate][:].bitcast(I32), w_in[gate][0][0].rearrange("p n t -> p (n t)").bitcast(I32))
+                )
+
+            small_loads = [
+                (mi_sb[:], Mi.flatten_outer_dims()),
+                (m_sb[:], m.flatten_outer_dims()),
+                (ci_sb[:], Ci.flatten_outer_dims()),
+                (ni_sb[:], Ni.flatten_outer_dims()),
+            ]
+            small_loads.extend(w_scale_loads(GATE_ORDER[0]))
+            for gate in GATE_ORDER:
+                small_loads.append((bias_rows[0:1, bias_cols[gate]], w_in[gate][2].unsqueeze(0)))
+                small_loads.append((bias_rows[1:2, bias_cols[gate]], r_in[gate][2].unsqueeze(0)))
+            for gate in GATE_ORDER[1:]:
+                small_loads.extend(w_scale_loads(gate))
+
+            for i, (dst, src) in enumerate(big_loads):
+                nc.sync.dma_start(out=dst, in_=src)
+                for small_dst, small_src in small_loads[SMALL_PER_BIG * i : SMALL_PER_BIG * (i + 1)]:
+                    nc.sync.dma_start(out=small_dst, in_=small_src)
+
+            def quantise(x_sb, n_groups, first_group):
+                words = x_sb[:].bitcast(F32)
+                grouped = stage.tile([P, n_groups * K_PASS], BF16, tag="grouped", align_bytes=64)
+                grouped_words = grouped[:].bitcast(F32).rearrange("p (g r u) -> p g r u", g=n_groups, u=PAIR)
+                in_bank = min(2, n_groups)
+                for b in range(n_groups // in_bank):
+                    bank = spare.tile([P, in_bank, PAIR, P], F32, tag="spare")
+                    for j in range(in_bank):
+                        g = in_bank * b + j
+                        for u in range(PAIR):
+                            nc.tensor.transpose(
+                                bank[:, j, u, :], words[:, 256 * g + u : 256 * (g + 1) : PAIR], ident[:]
+                            )
+                    dst = grouped_words[:, in_bank * b : in_bank * (b + 1)]
+                    src = bank[:].rearrange("p g u r -> p g r u")
+                    if b % 2 == 0:
+                        nc.vector.tensor_copy(out=dst, in_=src)
+                    else:
+                        nc.scalar.copy(out=dst, in_=src)
+                groups = slice(first_group, first_group + n_groups)
+                nc.vector.quantize_mx(
+                    out=x_codes[:, groups, :].rearrange("p g r -> p (g r)").bitcast(FP8X4),
+                    scales=x_scales[:, groups, :].rearrange("p g r -> p (g r)"),
+                    in_=grouped[:],
+                )
+
+            for c, zi_chunk in enumerate(zi_sb):
+                quantise(zi_chunk, CHUNK, CHUNK * c)
+            quantise(hi_sb, 1, HI_GROUP)
+
+        work = ctx.enter_context(tc.tile_pool(name="work", bufs=1))
+
+        def f32_tile(name):
+            return work.tile([P, DFF], F32, name=name)
 
         def gate_products(gate):
             acc = acc_pool.tile([P, DFF], F32, name="acc_%s" % gate)
@@ -171,7 +192,7 @@ def tile_customlstmcell_k_kernel(
                     lhsT=x_codes[:, g, :].bitcast(FP8X4),
                     lhsT_scale=x_scales[:, g, :],
                     rhs=r_words[gate][g // CHUNK][:, g % CHUNK, :].bitcast(FP8X4),
-                    rhs_scale=r_planes[first:P, g, :],
+                    rhs_scale=r_planes[gate][first:P, g, :],
                     start=(g == 0),
                     stop=False,
                 )
@@ -180,14 +201,11 @@ def tile_customlstmcell_k_kernel(
                 lhsT=x_codes[:, HI_GROUP, :].bitcast(FP8X4),
                 lhsT_scale=x_scales[:, HI_GROUP, :],
                 rhs=w_words[gate][:].bitcast(FP8X4),
-                rhs_scale=w_planes[first:P, :],
+                rhs_scale=w_planes[gate][first:P, :],
                 start=False,
                 stop=True,
             )
             return acc
-
-        def f32_tile(name):
-            return keep.tile([P, DFF], F32, name=name)
 
         acc_i = gate_products("I")
 
@@ -200,11 +218,11 @@ def tile_customlstmcell_k_kernel(
                 nc.vector.tensor_add(out=pre[gate][:], in0=bias_bank[:], in1=mi_sb[:])
             else:
                 nc.scalar.copy(out=pre[gate][:], in_=bias_bank[:])
-        m_f32 = keep.tile([P, 1], F32)
+        m_f32 = work.tile([P, 1], F32)
         nc.vector.tensor_copy(out=m_f32[:], in_=m_sb[:])
-        one_minus_m = keep.tile([P, 1], F32)
+        one_minus_m = work.tile([P, 1], F32)
         nc.vector.tensor_scalar(out=one_minus_m[:], in0=m_f32[:], scalar1=-1.0, scalar2=1.0, op0=ALU.mult, op1=ALU.add)
-        half_m = keep.tile([P, 1], F32)
+        half_m = work.tile([P, 1], F32)
         nc.vector.tensor_scalar_mul(out=half_m[:], in0=m_f32[:], scalar1=0.5)
         ci_m = f32_tile("ci_m")
         nc.vector.tensor_scalar_mul(out=ci_m[:], in0=ci_sb[:], scalar1=m_f32[:, 0:1])

@@ -98,10 +98,10 @@ def tile_customlstmcell_k_kernel(
         x_scales = keep.tile([P, Z_GROUPS + 1, P], U8, align_bytes=64)
 
         for gate in GATE_ORDER:
-            for quad in range(QUADRANTS):
+            for r in range(LIVE):
                 nc.gpsimd.dma_start(
-                    out=r_planes[gate][live_rows(gate, quad), :, :].bitcast(F32),
-                    in_=r_in[gate][1][:, LIVE * quad : LIVE * (quad + 1), :].rearrange("g r n -> r g n").bitcast(F32),
+                    out=r_planes[gate][plane_start[gate] + r : P : 32, :, :].bitcast(F32),
+                    in_=r_in[gate][1][:, r : 4 * QUADRANTS : LIVE, :].rearrange("g q n -> q g n").bitcast(F32),
                 )
 
         def w_scale_loads(gate):

@@ -24,7 +24,7 @@ N_CHUNKS = Z_GROUPS // CHUNK
 PAIR = 2
 QUADRANTS = 4
 LIVE = 4
-SMALL_PER_BIG = 2
+ROWS_PER_LOAD = 4
 
 GATE_ORDER = ("I", "F", "Z", "O")
 
@@ -70,9 +70,9 @@ def tile_customlstmcell_k_kernel(
         bias_rows = keep.tile([P, 4 * DFF], BF16)
         ones = keep.tile([P, P], BF16)
         ident = keep.tile([P, P], F32)
+        nc.vector.memset(r_planes[GATE_ORDER[0]][:].bitcast(I32), 0)
         for gate in GATE_ORDER:
             nc.vector.memset(w_planes[gate][:].bitcast(I32), 0)
-        nc.vector.memset(r_planes[GATE_ORDER[0]][:].bitcast(I32), 0)
         nc.vector.memset(bias_rows[:], 0.0)
         nc.vector.memset(ones[:], 1.0)
         for gate in GATE_ORDER[1:]:
@@ -97,18 +97,22 @@ def tile_customlstmcell_k_kernel(
         x_codes = keep.tile([P, Z_GROUPS + 1, P], U32, align_bytes=64)
         x_scales = keep.tile([P, Z_GROUPS + 1, P], U8, align_bytes=64)
 
-        for gate in GATE_ORDER:
-            for r in range(LIVE):
-                nc.gpsimd.dma_start(
-                    out=r_planes[gate][plane_start[gate] + r : P : 32, :, :].bitcast(F32),
-                    in_=r_in[gate][1][:, r : 4 * QUADRANTS : LIVE, :].rearrange("g q n -> q g n").bitcast(F32),
+        def scale_row_loads(gate):
+            return [
+                (
+                    r_planes[gate][row : row + 1, :, :].bitcast(I32),
+                    r_in[gate][1][:, LIVE * quad + r : LIVE * quad + r + 1, :].rearrange("g r n -> r g n").bitcast(I32),
                 )
+                for quad in range(QUADRANTS)
+                for r in range(LIVE)
+                for row in (32 * quad + plane_start[gate] + r,)
+            ]
 
         def w_scale_loads(gate):
             return [
                 (
-                    w_planes[gate][live_rows(gate, quad), :].bitcast(I32),
-                    w_in[gate][1][0, LIVE * quad : LIVE * (quad + 1), :].bitcast(I32),
+                    w_planes[gate][live_rows(gate, quad), :].bitcast(F32),
+                    w_in[gate][1][0, LIVE * quad : LIVE * (quad + 1), :].bitcast(F32),
                 )
                 for quad in range(QUADRANTS)
             ]
@@ -119,7 +123,6 @@ def tile_customlstmcell_k_kernel(
             big_loads = []
             for c, zi_chunk in enumerate(zi_sb):
                 big_loads.append((zi_chunk[:], zi_rows[:, CHUNK * K_PASS * c : CHUNK * K_PASS * (c + 1)]))
-            big_loads.append((hi_sb[:], Hi.flatten_outer_dims()))
             for gate in GATE_ORDER:
                 by_partition = r_in[gate][0].rearrange("g p n t -> p g (n t)")
                 for c, chunk in enumerate(r_words[gate]):
@@ -129,24 +132,27 @@ def tile_customlstmcell_k_kernel(
                 big_loads.append(
                     (w_words[gate][:].bitcast(I32), w_in[gate][0][0].rearrange("p n t -> p (n t)").bitcast(I32))
                 )
+                if gate == GATE_ORDER[0]:
+                    big_loads.append((hi_sb[:], Hi.flatten_outer_dims()))
+                    big_loads.append((mi_sb[:], Mi.flatten_outer_dims()))
+                    big_loads.append((ni_sb[:], Ni.flatten_outer_dims()))
+                    big_loads.append((ci_sb[:], Ci.flatten_outer_dims()))
+                    big_loads.append((m_sb[:], m.flatten_outer_dims()))
+            row_loads = [load for gate in GATE_ORDER for load in scale_row_loads(gate)]
 
-            small_loads = [
-                (mi_sb[:], Mi.flatten_outer_dims()),
-                (m_sb[:], m.flatten_outer_dims()),
-                (ci_sb[:], Ci.flatten_outer_dims()),
-                (ni_sb[:], Ni.flatten_outer_dims()),
-            ]
-            small_loads.extend(w_scale_loads(GATE_ORDER[0]))
+            with tc.manual_schedule(engines={mybir.EngineType.SP}):
+                for i, (dst, src) in enumerate(big_loads):
+                    nc.sync.dma_start(out=dst, in_=src)
+                    first_row = ROWS_PER_LOAD * (i - 1)
+                    if first_row >= 0:
+                        for row_dst, row_src in row_loads[first_row : first_row + ROWS_PER_LOAD]:
+                            nc.sync.dma_start(out=row_dst, in_=row_src)
+
             for gate in GATE_ORDER:
-                small_loads.append((bias_rows[0:1, bias_cols[gate]], w_in[gate][2].unsqueeze(0)))
-                small_loads.append((bias_rows[1:2, bias_cols[gate]], r_in[gate][2].unsqueeze(0)))
-            for gate in GATE_ORDER[1:]:
-                small_loads.extend(w_scale_loads(gate))
-
-            for i, (dst, src) in enumerate(big_loads):
-                nc.sync.dma_start(out=dst, in_=src)
-                for small_dst, small_src in small_loads[SMALL_PER_BIG * i : SMALL_PER_BIG * (i + 1)]:
-                    nc.sync.dma_start(out=small_dst, in_=small_src)
+                for dst, src in w_scale_loads(gate):
+                    nc.gpsimd.dma_start(out=dst, in_=src)
+                nc.gpsimd.dma_start(out=bias_rows[0:1, bias_cols[gate]], in_=w_in[gate][2].unsqueeze(0))
+                nc.gpsimd.dma_start(out=bias_rows[1:2, bias_cols[gate]], in_=r_in[gate][2].unsqueeze(0))
 
             def quantise(x_sb, n_groups, first_group):
                 words = x_sb[:].bitcast(F32)
@@ -237,7 +243,7 @@ def tile_customlstmcell_k_kernel(
         nc.vector.tensor_add(out=pre["F"][:], in0=acc_f[:], in1=pre["F"][:])
         m_t = f32_tile("m_t")
         nc.vector.tensor_max(out=m_t[:], in0=pre["F"][:], in1=pre["I"][:])
-        nc.sync.dma_start(out=out_1.flatten_outer_dims(), in_=m_t[:])
+        nc.gpsimd.dma_start(out=out_1.flatten_outer_dims(), in_=m_t[:])
         i_t = f32_tile("i_t")
         nc.vector.tensor_sub(out=i_t[:], in0=pre["I"][:], in1=m_t[:])
         nc.scalar.activation(out=i_t[:], in_=i_t[:], func=ACT.Exp)
@@ -247,7 +253,7 @@ def tile_customlstmcell_k_kernel(
         n_t = f32_tile("n_t")
         nc.vector.tensor_mul(out=n_t[:], in0=f_t[:], in1=ni_sb[:])
         nc.vector.tensor_add(out=n_t[:], in0=n_t[:], in1=i_t[:])
-        nc.sync.dma_start(out=out_3.flatten_outer_dims(), in_=n_t[:])
+        nc.gpsimd.dma_start(out=out_3.flatten_outer_dims(), in_=n_t[:])
         one_over_n = f32_tile("one_over_n")
         nc.vector.reciprocal(out=one_over_n[:], in_=n_t[:])
         c_t = f32_tile("c_t")
@@ -262,7 +268,7 @@ def tile_customlstmcell_k_kernel(
         nc.vector.scalar_tensor_tensor(
             out=c_t[:], in0=pre["Z"][:], scalar=m_f32[:, 0:1], in1=c_t[:], op0=ALU.mult, op1=ALU.add
         )
-        nc.sync.dma_start(out=out_0.flatten_outer_dims(), in_=c_t[:])
+        nc.gpsimd.dma_start(out=out_0.flatten_outer_dims(), in_=c_t[:])
         h_gain = f32_tile("h_gain")
         nc.vector.scalar_tensor_tensor(
             out=h_gain[:], in0=c_t[:], scalar=half_m[:, 0:1], in1=one_over_n[:], op0=ALU.mult, op1=ALU.mult

@@ -20,6 +20,7 @@ DFF = 512
 Z_GROUPS = D // K_PASS
 HI_GROUP = Z_GROUPS
 CHUNK = 4
+ZI_LOADS = 2
 N_CHUNKS = Z_GROUPS // CHUNK
 PAIR = 2
 QUADRANTS = 4
@@ -108,54 +109,65 @@ def tile_customlstmcell_k_kernel(
                 for row in (32 * quad + plane_start[gate] + r,)
             ]
 
-        def w_scale_loads(gate):
+        def w_scale_loads(gate, view):
             return [
                 (
-                    w_planes[gate][live_rows(gate, quad), :].bitcast(F32),
-                    w_in[gate][1][0, LIVE * quad : LIVE * (quad + 1), :].bitcast(F32),
+                    w_planes[gate][live_rows(gate, quad), :].bitcast(view),
+                    w_in[gate][1][0, LIVE * quad : LIVE * (quad + 1), :].bitcast(view),
                 )
                 for quad in range(QUADRANTS)
             ]
 
         with tc.tile_pool(name="x_rows", bufs=1) as x_rows, tc.tile_pool(name="stage", bufs=2) as stage:
             zi_rows = Zi.flatten_outer_dims()
-            zi_sb = [x_rows.tile([P, CHUNK * K_PASS], BF16, name="zi_sb%d" % c) for c in range(N_CHUNKS)]
+            zi_cols = D // ZI_LOADS
+            zi_sb = [x_rows.tile([P, zi_cols], BF16, name="zi_sb%d" % c) for c in range(ZI_LOADS)]
             big_loads = []
-            for c, zi_chunk in enumerate(zi_sb):
-                big_loads.append((zi_chunk[:], zi_rows[:, CHUNK * K_PASS * c : CHUNK * K_PASS * (c + 1)]))
             for gate in GATE_ORDER:
                 by_partition = r_in[gate][0].rearrange("g p n t -> p g (n t)")
                 for c, chunk in enumerate(r_words[gate]):
                     big_loads.append(
                         (chunk[:].bitcast(I32), by_partition[:, CHUNK * c : CHUNK * (c + 1), :].bitcast(I32))
                     )
-                big_loads.append(
-                    (w_words[gate][:].bitcast(I32), w_in[gate][0][0].rearrange("p n t -> p (n t)").bitcast(I32))
-                )
-                if gate == GATE_ORDER[0]:
-                    big_loads.append((hi_sb[:], Hi.flatten_outer_dims()))
-                    big_loads.append((mi_sb[:], Mi.flatten_outer_dims()))
-                    big_loads.append((ni_sb[:], Ni.flatten_outer_dims()))
-                    big_loads.append((ci_sb[:], Ci.flatten_outer_dims()))
-                    big_loads.append((m_sb[:], m.flatten_outer_dims()))
-            row_loads = [load for gate in GATE_ORDER for load in scale_row_loads(gate)]
+            row_loads = [load for gate in GATE_ORDER[1:] for load in scale_row_loads(gate)]
 
             with tc.manual_schedule(engines={mybir.EngineType.SP}):
+                row_inputs = [(mi_sb, Mi), (m_sb, m), (ci_sb, Ci), (ni_sb, Ni)]
+                for c, zi_part in enumerate(zi_sb):
+                    nc.sync.dma_start(out=zi_part[:], in_=zi_rows[:, zi_cols * c : zi_cols * (c + 1)])
+                    for dst, src in row_inputs[2 * c : 2 * (c + 1)]:
+                        nc.sync.dma_start(out=dst[:], in_=src.flatten_outer_dims())
                 for i, (dst, src) in enumerate(big_loads):
                     nc.sync.dma_start(out=dst, in_=src)
-                    first_row = ROWS_PER_LOAD * (i - 1)
-                    if first_row >= 0:
-                        for row_dst, row_src in row_loads[first_row : first_row + ROWS_PER_LOAD]:
-                            nc.sync.dma_start(out=row_dst, in_=row_src)
+                    for row_dst, row_src in row_loads[ROWS_PER_LOAD * i : ROWS_PER_LOAD * (i + 1)]:
+                        nc.sync.dma_start(out=row_dst, in_=row_src)
+                    if i % N_CHUNKS == N_CHUNKS - 1:
+                        gate = GATE_ORDER[i // N_CHUNKS]
+                        nc.sync.dma_start(
+                            out=w_words[gate][:].bitcast(I32),
+                            in_=w_in[gate][0][0].rearrange("p n t -> p (n t)").bitcast(I32),
+                        )
+                        if gate in GATE_ORDER[2:]:
+                            for small_dst, small_src in w_scale_loads(gate, I32):
+                                nc.sync.dma_start(out=small_dst, in_=small_src)
 
+            first_gate = GATE_ORDER[0]
+            for r in range(LIVE):
+                nc.gpsimd.dma_start(
+                    out=r_planes[first_gate][plane_start[first_gate] + r : P : 32, :, :].bitcast(F32),
+                    in_=r_in[first_gate][1][:, r : 4 * QUADRANTS : LIVE, :].rearrange("g q n -> q g n").bitcast(F32),
+                )
+            small_loads = [(hi_sb[:], Hi.flatten_outer_dims())]
+            small_loads.extend(w_scale_loads(GATE_ORDER[0], F32))
             for gate in GATE_ORDER:
-                for dst, src in w_scale_loads(gate):
-                    nc.gpsimd.dma_start(out=dst, in_=src)
-                nc.gpsimd.dma_start(out=bias_rows[0:1, bias_cols[gate]], in_=w_in[gate][2].unsqueeze(0))
-                nc.gpsimd.dma_start(out=bias_rows[1:2, bias_cols[gate]], in_=r_in[gate][2].unsqueeze(0))
+                small_loads.append((bias_rows[0:1, bias_cols[gate]], w_in[gate][2].unsqueeze(0)))
+                small_loads.append((bias_rows[1:2, bias_cols[gate]], r_in[gate][2].unsqueeze(0)))
+            small_loads.extend(w_scale_loads(GATE_ORDER[1], F32))
+            for dst, src in small_loads:
+                nc.gpsimd.dma_start(out=dst, in_=src)
 
             def quantise(x_sb, n_groups, first_group):
-                words = x_sb[:].bitcast(F32)
+                words = x_sb.bitcast(F32)
                 grouped = stage.tile([P, n_groups * K_PASS], BF16, tag="grouped", align_bytes=64)
                 grouped_words = grouped[:].bitcast(F32).rearrange("p (g r u) -> p g r u", g=n_groups, u=PAIR)
                 in_bank = min(2, n_groups)
@@ -180,9 +192,10 @@ def tile_customlstmcell_k_kernel(
                     in_=grouped[:],
                 )
 
-            for c, zi_chunk in enumerate(zi_sb):
-                quantise(zi_chunk, CHUNK, CHUNK * c)
-            quantise(hi_sb, 1, HI_GROUP)
+            for c in range(N_CHUNKS):
+                load, part = divmod(c, N_CHUNKS // ZI_LOADS)
+                quantise(zi_sb[load][:, CHUNK * K_PASS * part : CHUNK * K_PASS * (part + 1)], CHUNK, CHUNK * c)
+            quantise(hi_sb[:], 1, HI_GROUP)
 
         work = ctx.enter_context(tc.tile_pool(name="work", bufs=1))
 

@@ -25,7 +25,6 @@ N_CHUNKS = Z_GROUPS // CHUNK
 PAIR = 2
 QUADRANTS = 4
 LIVE = 4
-ROWS_PER_LOAD = 4
 
 GATE_ORDER = ("I", "F", "Z", "O")
 
@@ -64,20 +63,16 @@ def tile_customlstmcell_k_kernel(
         acc_pool = ctx.enter_context(tc.psum_pool(name="acc", bufs=1))
         spare = ctx.enter_context(tc.psum_pool(name="spare", bufs=4))
 
-        r_planes = {
-            gate: keep.tile([P, Z_GROUPS, DFF], U8, name="r_planes_%s" % gate, align_bytes=64) for gate in GATE_ORDER
-        }
+        r_planes = keep.tile([P, Z_GROUPS, DFF], U8, align_bytes=64)
         w_planes = {gate: keep.tile([P, DFF], U8, name="w_planes_%s" % gate, align_bytes=64) for gate in GATE_ORDER}
         bias_rows = keep.tile([P, 4 * DFF], BF16)
         ones = keep.tile([P, P], BF16)
         ident = keep.tile([P, P], F32)
-        nc.vector.memset(r_planes[GATE_ORDER[0]][:].bitcast(I32), 0)
+        nc.vector.memset(r_planes[:].bitcast(I32), 0)
         for gate in GATE_ORDER:
             nc.vector.memset(w_planes[gate][:].bitcast(I32), 0)
         nc.vector.memset(bias_rows[:], 0.0)
         nc.vector.memset(ones[:], 1.0)
-        for gate in GATE_ORDER[1:]:
-            nc.vector.memset(r_planes[gate][:].bitcast(I32), 0)
         make_identity(nc, ident[:])
 
         r_words = {
@@ -98,22 +93,11 @@ def tile_customlstmcell_k_kernel(
         x_codes = keep.tile([P, Z_GROUPS + 1, P], U32, align_bytes=64)
         x_scales = keep.tile([P, Z_GROUPS + 1, P], U8, align_bytes=64)
 
-        def scale_row_loads(gate):
+        def w_scale_loads(gate):
             return [
                 (
-                    r_planes[gate][row : row + 1, :, :].bitcast(I32),
-                    r_in[gate][1][:, LIVE * quad + r : LIVE * quad + r + 1, :].rearrange("g r n -> r g n").bitcast(I32),
-                )
-                for quad in range(QUADRANTS)
-                for r in range(LIVE)
-                for row in (32 * quad + plane_start[gate] + r,)
-            ]
-
-        def w_scale_loads(gate, view):
-            return [
-                (
-                    w_planes[gate][live_rows(gate, quad), :].bitcast(view),
-                    w_in[gate][1][0, LIVE * quad : LIVE * (quad + 1), :].bitcast(view),
+                    w_planes[gate][live_rows(gate, quad), :].bitcast(F32),
+                    w_in[gate][1][0, LIVE * quad : LIVE * (quad + 1), :].bitcast(F32),
                 )
                 for quad in range(QUADRANTS)
             ]
@@ -129,40 +113,34 @@ def tile_customlstmcell_k_kernel(
                     big_loads.append(
                         (chunk[:].bitcast(I32), by_partition[:, CHUNK * c : CHUNK * (c + 1), :].bitcast(I32))
                     )
-            row_loads = [load for gate in GATE_ORDER[1:] for load in scale_row_loads(gate)]
 
             with tc.manual_schedule(engines={mybir.EngineType.SP}):
-                row_inputs = [(mi_sb, Mi), (m_sb, m), (ci_sb, Ci), (ni_sb, Ni)]
+                for r in range(LIVE):
+                    for gate in GATE_ORDER:
+                        nc.sync.dma_start(
+                            out=r_planes[plane_start[gate] + r : P : 32, :, :].bitcast(I32),
+                            in_=r_in[gate][1][:, r : 4 * QUADRANTS : LIVE, :].rearrange("g q n -> q g n").bitcast(I32),
+                        )
+                row_inputs = [(hi_sb, Hi), (mi_sb, Mi), (m_sb, m), (ci_sb, Ci), (ni_sb, Ni)]
                 for c, zi_part in enumerate(zi_sb):
                     nc.sync.dma_start(out=zi_part[:], in_=zi_rows[:, zi_cols * c : zi_cols * (c + 1)])
-                    for dst, src in row_inputs[2 * c : 2 * (c + 1)]:
-                        nc.sync.dma_start(out=dst[:], in_=src.flatten_outer_dims())
                 for i, (dst, src) in enumerate(big_loads):
                     nc.sync.dma_start(out=dst, in_=src)
-                    for row_dst, row_src in row_loads[ROWS_PER_LOAD * i : ROWS_PER_LOAD * (i + 1)]:
-                        nc.sync.dma_start(out=row_dst, in_=row_src)
+                    for row_dst, row_src in row_inputs[i : i + 1]:
+                        nc.sync.dma_start(out=row_dst[:], in_=row_src.flatten_outer_dims())
                     if i % N_CHUNKS == N_CHUNKS - 1:
                         gate = GATE_ORDER[i // N_CHUNKS]
                         nc.sync.dma_start(
                             out=w_words[gate][:].bitcast(I32),
                             in_=w_in[gate][0][0].rearrange("p n t -> p (n t)").bitcast(I32),
                         )
-                        if gate in GATE_ORDER[2:]:
-                            for small_dst, small_src in w_scale_loads(gate, I32):
-                                nc.sync.dma_start(out=small_dst, in_=small_src)
 
-            first_gate = GATE_ORDER[0]
-            for r in range(LIVE):
-                nc.gpsimd.dma_start(
-                    out=r_planes[first_gate][plane_start[first_gate] + r : P : 32, :, :].bitcast(F32),
-                    in_=r_in[first_gate][1][:, r : 4 * QUADRANTS : LIVE, :].rearrange("g q n -> q g n").bitcast(F32),
-                )
-            small_loads = [(hi_sb[:], Hi.flatten_outer_dims())]
-            small_loads.extend(w_scale_loads(GATE_ORDER[0], F32))
+            small_loads = []
             for gate in GATE_ORDER:
                 small_loads.append((bias_rows[0:1, bias_cols[gate]], w_in[gate][2].unsqueeze(0)))
                 small_loads.append((bias_rows[1:2, bias_cols[gate]], r_in[gate][2].unsqueeze(0)))
-            small_loads.extend(w_scale_loads(GATE_ORDER[1], F32))
+            for gate in GATE_ORDER:
+                small_loads.extend(w_scale_loads(gate))
             for dst, src in small_loads:
                 nc.gpsimd.dma_start(out=dst, in_=src)
 
@@ -211,7 +189,7 @@ def tile_customlstmcell_k_kernel(
                     lhsT=x_codes[:, g, :].bitcast(FP8X4),
                     lhsT_scale=x_scales[:, g, :],
                     rhs=r_words[gate][g // CHUNK][:, g % CHUNK, :].bitcast(FP8X4),
-                    rhs_scale=r_planes[gate][first:P, g, :],
+                    rhs_scale=r_planes[first:P, g, :],
                     start=(g == 0),
                     stop=False,
                 )

@@ -22,11 +22,16 @@ HI_GROUP = Z_GROUPS
 CHUNK = 4
 ZI_LOADS = 2
 N_CHUNKS = Z_GROUPS // CHUNK
+HALF = DFF // 2
 PAIR = 2
 QUADRANTS = 4
 LIVE = 4
+SMALL_PER_BIG = 2
 
 GATE_ORDER = ("I", "F", "Z", "O")
+
+LOAD_GROUPS = {gate: (CHUNK,) * N_CHUNKS for gate in GATE_ORDER[:-1]}
+LOAD_GROUPS[GATE_ORDER[-1]] = (CHUNK,) * (N_CHUNKS - 1) + (CHUNK - 1, 1)
 
 FLOPS = 2 * P * (D + DFF) * 4 * DFF
 
@@ -77,8 +82,8 @@ def tile_customlstmcell_k_kernel(
 
         r_words = {
             gate: [
-                keep.tile([P, CHUNK, PACK * DFF], U8, name="r_words_%s%d" % (gate, c), align_bytes=64)
-                for c in range(N_CHUNKS)
+                keep.tile([P, n, PACK * DFF], U8, name="r_words_%s%d" % (gate, c), align_bytes=64)
+                for c, n in enumerate(LOAD_GROUPS[gate])
             ]
             for gate in GATE_ORDER
         }
@@ -96,8 +101,8 @@ def tile_customlstmcell_k_kernel(
         def w_scale_loads(gate):
             return [
                 (
-                    w_planes[gate][live_rows(gate, quad), :].bitcast(F32),
-                    w_in[gate][1][0, LIVE * quad : LIVE * (quad + 1), :].bitcast(F32),
+                    w_planes[gate][live_rows(gate, quad), :].bitcast(I32),
+                    w_in[gate][1][0, LIVE * quad : LIVE * (quad + 1), :].bitcast(I32),
                 )
                 for quad in range(QUADRANTS)
             ]
@@ -109,40 +114,50 @@ def tile_customlstmcell_k_kernel(
             big_loads = []
             for gate in GATE_ORDER:
                 by_partition = r_in[gate][0].rearrange("g p n t -> p g (n t)")
-                for c, chunk in enumerate(r_words[gate]):
+                first_group = 0
+                for chunk, n in zip(r_words[gate], LOAD_GROUPS[gate]):
                     big_loads.append(
-                        (chunk[:].bitcast(I32), by_partition[:, CHUNK * c : CHUNK * (c + 1), :].bitcast(I32))
+                        (
+                            chunk[:].bitcast(I32),
+                            by_partition[:, first_group : first_group + n, :].bitcast(I32),
+                            SMALL_PER_BIG if n == CHUNK else 0,
+                        )
                     )
+                    first_group += n
+                    if first_group == CHUNK:
+                        big_loads.append(
+                            (
+                                w_words[gate][:].bitcast(I32),
+                                w_in[gate][0][0].rearrange("p n t -> p (n t)").bitcast(I32),
+                                0,
+                            )
+                        )
+
+            row_inputs = {
+                "I": [(hi_sb, Hi)], "F": [(mi_sb, Mi), (m_sb, m), (ci_sb, Ci), (ni_sb, Ni)], "Z": [], "O": []
+            }
+            small_loads = []
+            for gate in GATE_ORDER:
+                small_loads.extend((dst[:], src.flatten_outer_dims()) for dst, src in row_inputs[gate])
+                small_loads.extend(w_scale_loads(gate))
+                small_loads.append((bias_rows[0:1, bias_cols[gate]], w_in[gate][2].unsqueeze(0)))
+                small_loads.append((bias_rows[1:2, bias_cols[gate]], r_in[gate][2].unsqueeze(0)))
+            waiting = list(reversed(small_loads))
 
             with tc.manual_schedule(engines={mybir.EngineType.SP}):
+                nc.sync.dma_start(out=zi_sb[0][:], in_=zi_rows[:, :zi_cols])
                 for r in range(LIVE):
                     for gate in GATE_ORDER:
                         nc.sync.dma_start(
                             out=r_planes[plane_start[gate] + r : P : 32, :, :].bitcast(I32),
                             in_=r_in[gate][1][:, r : 4 * QUADRANTS : LIVE, :].rearrange("g q n -> q g n").bitcast(I32),
                         )
-                row_inputs = [(hi_sb, Hi), (mi_sb, Mi), (m_sb, m), (ci_sb, Ci), (ni_sb, Ni)]
-                for c, zi_part in enumerate(zi_sb):
-                    nc.sync.dma_start(out=zi_part[:], in_=zi_rows[:, zi_cols * c : zi_cols * (c + 1)])
-                for i, (dst, src) in enumerate(big_loads):
+                big_loads.insert(0, (zi_sb[1][:], zi_rows[:, zi_cols:], 1 + QUADRANTS))
+                for dst, src, n in big_loads:
                     nc.sync.dma_start(out=dst, in_=src)
-                    for row_dst, row_src in row_inputs[i : i + 1]:
-                        nc.sync.dma_start(out=row_dst[:], in_=row_src.flatten_outer_dims())
-                    if i % N_CHUNKS == N_CHUNKS - 1:
-                        gate = GATE_ORDER[i // N_CHUNKS]
-                        nc.sync.dma_start(
-                            out=w_words[gate][:].bitcast(I32),
-                            in_=w_in[gate][0][0].rearrange("p n t -> p (n t)").bitcast(I32),
-                        )
-
-            small_loads = []
-            for gate in GATE_ORDER:
-                small_loads.append((bias_rows[0:1, bias_cols[gate]], w_in[gate][2].unsqueeze(0)))
-                small_loads.append((bias_rows[1:2, bias_cols[gate]], r_in[gate][2].unsqueeze(0)))
-            for gate in GATE_ORDER:
-                small_loads.extend(w_scale_loads(gate))
-            for dst, src in small_loads:
-                nc.gpsimd.dma_start(out=dst, in_=src)
+                    for i in range(min(n, len(waiting))):
+                        small_dst, small_src = waiting.pop()
+                        nc.sync.dma_start(out=small_dst, in_=small_src)
 
             def quantise(x_sb, n_groups, first_group):
                 words = x_sb.bitcast(F32)
@@ -183,31 +198,34 @@ def tile_customlstmcell_k_kernel(
         def gate_products(gate):
             acc = acc_pool.tile([P, DFF], F32, name="acc_%s" % gate)
             first = plane_start[gate]
-            for g in range(Z_GROUPS):
+            slots = [(chunk, j) for chunk, n in zip(r_words[gate], LOAD_GROUPS[gate]) for j in range(n)]
+            for g, (chunk, j) in enumerate(slots):
                 nc.tensor.matmul_mx(
                     out=acc[:],
                     lhsT=x_codes[:, g, :].bitcast(FP8X4),
                     lhsT_scale=x_scales[:, g, :],
-                    rhs=r_words[gate][g // CHUNK][:, g % CHUNK, :].bitcast(FP8X4),
+                    rhs=chunk[:, j, :].bitcast(FP8X4),
                     rhs_scale=r_planes[first:P, g, :],
                     start=(g == 0),
-                    stop=False,
+                    stop=(g == Z_GROUPS - 1),
                 )
-            nc.tensor.matmul_mx(
-                out=acc[:],
-                lhsT=x_codes[:, HI_GROUP, :].bitcast(FP8X4),
-                lhsT_scale=x_scales[:, HI_GROUP, :],
-                rhs=w_words[gate][:].bitcast(FP8X4),
-                rhs_scale=w_planes[gate][first:P, :],
-                start=False,
-                stop=True,
-            )
+                if g == CHUNK - 1:
+                    nc.tensor.matmul_mx(
+                        out=acc[:],
+                        lhsT=x_codes[:, HI_GROUP, :].bitcast(FP8X4),
+                        lhsT_scale=x_scales[:, HI_GROUP, :],
+                        rhs=w_words[gate][:].bitcast(FP8X4),
+                        rhs_scale=w_planes[gate][first:P, :],
+                        start=False,
+                        stop=False,
+                    )
             return acc
 
         acc_i = gate_products("I")
 
         pre = {}
-        for gate in GATE_ORDER:
+
+        def add_biases(gate):
             bias_bank = spare.tile([P, DFF], F32, tag="spare")
             nc.tensor.matmul(out=bias_bank[:], lhsT=ones[:], rhs=bias_rows[:, bias_cols[gate]], start=True, stop=True)
             pre[gate] = f32_tile("pre_%s" % gate)
@@ -215,6 +233,8 @@ def tile_customlstmcell_k_kernel(
                 nc.vector.tensor_add(out=pre[gate][:], in0=bias_bank[:], in1=mi_sb[:])
             else:
                 nc.scalar.copy(out=pre[gate][:], in_=bias_bank[:])
+        add_biases("I")
+        add_biases("F")
         m_f32 = work.tile([P, 1], F32)
         nc.vector.tensor_copy(out=m_f32[:], in_=m_sb[:])
         one_minus_m = work.tile([P, 1], F32)
@@ -251,6 +271,8 @@ def tile_customlstmcell_k_kernel(
         nc.vector.tensor_mul(out=c_t[:], in0=f_t[:], in1=ci_m[:])
         nc.vector.tensor_add(out=c_t[:], in0=c_t[:], in1=ci_keep[:])
 
+        add_biases("Z")
+        add_biases("O")
         acc_z = gate_products("Z")
 
         nc.vector.tensor_add(out=pre["Z"][:], in0=acc_z[:], in1=pre["Z"][:])
@@ -268,8 +290,14 @@ def tile_customlstmcell_k_kernel(
 
         acc_o = gate_products("O")
 
-        nc.vector.tensor_add(out=pre["O"][:], in0=acc_o[:], in1=pre["O"][:])
-        nc.scalar.activation(out=pre["O"][:], in_=pre["O"][:], func=ACT.Tanh, scale=0.5)
-        nc.vector.tensor_mul(out=pre["O"][:], in0=pre["O"][:], in1=h_gain[:])
-        nc.vector.tensor_add(out=pre["O"][:], in0=pre["O"][:], in1=h_rest[:])
-        nc.sync.dma_start(out=out_2.flatten_outer_dims(), in_=pre["O"][:])
+        halves = [slice(0, HALF), slice(HALF, DFF)]
+        h_t = [f32_tile("h_t%d" % i) for i in range(2)]
+        for out, cols in zip(h_t, halves):
+            nc.vector.tensor_add(out=out[:, :HALF], in0=acc_o[:, cols], in1=pre["O"][:, cols])
+        for out in h_t:
+            nc.scalar.activation(out=out[:, :HALF], in_=out[:, :HALF], func=ACT.Tanh, scale=0.5)
+        for out, cols in zip(h_t, halves):
+            nc.vector.tensor_mul(out=out[:, :HALF], in0=out[:, :HALF], in1=h_gain[:, cols])
+        for out, cols in zip(h_t, halves):
+            nc.vector.tensor_add(out=out[:, :HALF], in0=out[:, :HALF], in1=h_rest[:, cols])
+            nc.sync.dma_start(out=out_2.flatten_outer_dims()[:, cols], in_=out[:, :HALF])

@@ -144,14 +144,16 @@ def tile_customlstmcell_k_kernel(
                 small_loads.append((bias_rows[1:2, bias_cols[gate]], r_in[gate][2].unsqueeze(0)))
             waiting = list(reversed(small_loads))
 
-            with tc.manual_schedule(engines={mybir.EngineType.SP}):
+            with tc.manual_schedule(engines={mybir.EngineType.SP, mybir.EngineType.Activation}):
                 nc.sync.dma_start(out=zi_sb[0][:], in_=zi_rows[:, :zi_cols])
                 for r in range(LIVE):
-                    for gate in GATE_ORDER:
-                        nc.sync.dma_start(
-                            out=r_planes[plane_start[gate] + r : P : 32, :, :].bitcast(I32),
-                            in_=r_in[gate][1][:, r : 4 * QUADRANTS : LIVE, :].rearrange("g q n -> q g n").bitcast(I32),
-                        )
+                    for i, gate in enumerate(GATE_ORDER):
+                        dst = r_planes[plane_start[gate] + r : P : 32, :, :]
+                        src = r_in[gate][1][:, r : 4 * QUADRANTS : LIVE, :].rearrange("g q n -> q g n")
+                        if i % 2 == 0:
+                            nc.sync.dma_start(out=dst.bitcast(I32), in_=src.bitcast(I32))
+                        else:
+                            nc.scalar.dma_start(out=dst.bitcast(F32), in_=src.bitcast(F32))
                 big_loads.insert(0, (zi_sb[1][:], zi_rows[:, zi_cols:], 1 + QUADRANTS))
                 for dst, src, n in big_loads:
                     nc.sync.dma_start(out=dst, in_=src)

@@ -256,7 +256,7 @@ def tile_customlstmcell_k_kernel(
         nc.vector.tensor_add(out=pre["F"][:], in0=acc_f[:], in1=pre["F"][:])
         m_t = f32_tile("m_t")
         nc.vector.tensor_max(out=m_t[:], in0=pre["F"][:], in1=pre["I"][:])
-        nc.gpsimd.dma_start(out=out_1.flatten_outer_dims(), in_=m_t[:])
+        nc.sync.dma_start(out=out_1.flatten_outer_dims(), in_=m_t[:])
         i_t = f32_tile("i_t")
         nc.vector.tensor_sub(out=i_t[:], in0=pre["I"][:], in1=m_t[:])
         nc.scalar.activation(out=i_t[:], in_=i_t[:], func=ACT.Exp)
@@ -266,7 +266,7 @@ def tile_customlstmcell_k_kernel(
         n_t = f32_tile("n_t")
         nc.vector.tensor_mul(out=n_t[:], in0=f_t[:], in1=ni_sb[:])
         nc.vector.tensor_add(out=n_t[:], in0=n_t[:], in1=i_t[:])
-        nc.gpsimd.dma_start(out=out_3.flatten_outer_dims(), in_=n_t[:])
+        nc.sync.dma_start(out=out_3.flatten_outer_dims(), in_=n_t[:])
         one_over_n = f32_tile("one_over_n")
         nc.vector.reciprocal(out=one_over_n[:], in_=n_t[:])
         c_t = f32_tile("c_t")
@@ -283,7 +283,7 @@ def tile_customlstmcell_k_kernel(
         nc.vector.scalar_tensor_tensor(
             out=c_t[:], in0=pre["Z"][:], scalar=m_f32[:, 0:1], in1=c_t[:], op0=ALU.mult, op1=ALU.add
         )
-        nc.gpsimd.dma_start(out=out_0.flatten_outer_dims(), in_=c_t[:])
+        nc.sync.dma_start(out=out_0.flatten_outer_dims(), in_=c_t[:])
         h_gain = f32_tile("h_gain")
         nc.vector.scalar_tensor_tensor(
             out=h_gain[:], in0=c_t[:], scalar=half_m[:, 0:1], in1=one_over_n[:], op0=ALU.mult, op1=ALU.mult

@@ -26,12 +26,12 @@ HALF = DFF // 2
 PAIR = 2
 QUADRANTS = 4
 LIVE = 4
-SMALL_PER_BIG = 2
+SMALL_PER_BIG = 4
 
 GATE_ORDER = ("I", "F", "Z", "O")
 
-LOAD_GROUPS = {gate: (CHUNK,) * N_CHUNKS for gate in GATE_ORDER[:-1]}
-LOAD_GROUPS[GATE_ORDER[-1]] = (CHUNK,) * (N_CHUNKS - 1) + (CHUNK - 1, 1)
+LOAD_GROUPS = {gate: (8, 8) for gate in GATE_ORDER[:-1]}
+LOAD_GROUPS[GATE_ORDER[-1]] = (8, 4, 3, 1)
 
 FLOPS = 2 * P * (D + DFF) * 4 * DFF
 
@@ -70,7 +70,7 @@ def tile_customlstmcell_k_kernel(
 
         r_planes = keep.tile([P, Z_GROUPS, DFF], U8, align_bytes=64)
         w_planes = {gate: keep.tile([P, DFF], U8, name="w_planes_%s" % gate, align_bytes=64) for gate in GATE_ORDER}
-        bias_rows = keep.tile([P, 4 * DFF], BF16)
+        bias_rows = keep.tile([P, 4 * DFF + P], BF16)
         ones = keep.tile([P, P], BF16)
         ident = keep.tile([P, P], F32)
         nc.vector.memset(r_planes[:].bitcast(I32), 0)
@@ -94,7 +94,6 @@ def tile_customlstmcell_k_kernel(
         ci_sb = keep.tile([P, DFF], BF16)
         mi_sb = keep.tile([P, DFF], BF16)
         ni_sb = keep.tile([P, DFF], BF16)
-        m_sb = keep.tile([P, 1], BF16)
         x_codes = keep.tile([P, Z_GROUPS + 1, P], U32, align_bytes=64)
         x_scales = keep.tile([P, Z_GROUPS + 1, P], U8, align_bytes=64)
 
@@ -120,11 +119,11 @@ def tile_customlstmcell_k_kernel(
                         (
                             chunk[:].bitcast(I32),
                             by_partition[:, first_group : first_group + n, :].bitcast(I32),
-                            SMALL_PER_BIG if n == CHUNK else 0,
+                            SMALL_PER_BIG if n == LOAD_GROUPS[GATE_ORDER[0]][0] else 0,
                         )
                     )
                     first_group += n
-                    if first_group == CHUNK:
+                    if first_group == n:
                         big_loads.append(
                             (
                                 w_words[gate][:].bitcast(I32),
@@ -134,14 +133,17 @@ def tile_customlstmcell_k_kernel(
                         )
 
             row_inputs = {
-                "I": [(hi_sb, Hi)], "F": [(mi_sb, Mi), (m_sb, m), (ci_sb, Ci), (ni_sb, Ni)], "Z": [], "O": []
+                "I": [(hi_sb, Hi)], "F": [(mi_sb, Mi), (ci_sb, Ci), (ni_sb, Ni)], "Z": [], "O": []
             }
+            m_cols = slice(4 * DFF, 4 * DFF + P)
             small_loads = []
             for gate in GATE_ORDER:
                 small_loads.extend((dst[:], src.flatten_outer_dims()) for dst, src in row_inputs[gate])
                 small_loads.extend(w_scale_loads(gate))
                 small_loads.append((bias_rows[0:1, bias_cols[gate]], w_in[gate][2].unsqueeze(0)))
                 small_loads.append((bias_rows[1:2, bias_cols[gate]], r_in[gate][2].unsqueeze(0)))
+                if gate == "I":
+                    small_loads.append((bias_rows[0:1, m_cols], m.rearrange("b p one -> one (b p)")))
             waiting = list(reversed(small_loads))
 
             with tc.manual_schedule(engines={mybir.EngineType.SP, mybir.EngineType.Activation}):
@@ -211,7 +213,7 @@ def tile_customlstmcell_k_kernel(
                     start=(g == 0),
                     stop=(g == Z_GROUPS - 1),
                 )
-                if g == CHUNK - 1:
+                if g == LOAD_GROUPS[gate][0] - 1:
                     nc.tensor.matmul_mx(
                         out=acc[:],
                         lhsT=x_codes[:, HI_GROUP, :].bitcast(FP8X4),
@@ -237,8 +239,10 @@ def tile_customlstmcell_k_kernel(
                 nc.scalar.copy(out=pre[gate][:], in_=bias_bank[:])
         add_biases("I")
         add_biases("F")
+        m_bank = spare.tile([P, DFF], F32, tag="spare")
+        nc.tensor.matmul(out=m_bank[:, :32], lhsT=bias_rows[:, m_cols], rhs=ones[:, :32], start=True, stop=True)
         m_f32 = work.tile([P, 1], F32)
-        nc.vector.tensor_copy(out=m_f32[:], in_=m_sb[:])
+        nc.vector.tensor_copy(out=m_f32[:], in_=m_bank[:, 0:1])
         one_minus_m = work.tile([P, 1], F32)
         nc.vector.tensor_scalar(out=one_minus_m[:], in0=m_f32[:], scalar1=-1.0, scalar2=1.0, op0=ALU.mult, op1=ALU.add)
         half_m = work.tile([P, 1], F32)

from contextlib import ExitStack

import concourse.mybir as mybir
from concourse.masks import make_identity

BF16 = mybir.dt.bfloat16
F32 = mybir.dt.float32
I32 = mybir.dt.int32
U8 = mybir.dt.uint8
U32 = mybir.dt.uint32
FP8X4 = mybir.dt.float8_e4m3fn_x4
ALU = mybir.AluOpType
ACT = mybir.ActivationFunctionType

P = 128
PACK = 4
K_PASS = P * PACK
D = 8192
DFF = 512
Z_GROUPS = D // K_PASS
HI_GROUP = Z_GROUPS
CHUNK = 4
ZI_LOADS = 2
N_CHUNKS = Z_GROUPS // CHUNK
HALF = DFF // 2
PAIR = 2
QUADRANTS = 4
LIVE = 4
SMALL_PER_BIG = 4

GATE_ORDER = ("I", "F", "Z", "O")

LOAD_GROUPS = {gate: (8, 8) for gate in GATE_ORDER[:-1]}
LOAD_GROUPS[GATE_ORDER[-1]] = (8, 4, 3, 1)

FLOPS = 2 * P * (D + DFF) * 4 * DFF


def tile_customlstmcell_k_kernel(
    tc, Zi, Ci, Mi, Hi, Ni, m,
    WI_w_words, WI_w_scales, WI_b, WF_w_words, WF_w_scales, WF_b,
    WO_w_words, WO_w_scales, WO_b, WZ_w_words, WZ_w_scales, WZ_b,
    RI_w_words, RI_w_scales, RI_b, RF_w_words, RF_w_scales, RF_b,
    RO_w_words, RO_w_scales, RO_b, RZ_w_words, RZ_w_scales, RZ_b,
    out_0, out_1, out_2, out_3,
):
    nc = tc.nc
    w_in = {
        "I": (WI_w_words, WI_w_scales, WI_b),
        "F": (WF_w_words, WF_w_scales, WF_b),
        "O": (WO_w_words, WO_w_scales, WO_b),
        "Z": (WZ_w_words, WZ_w_scales, WZ_b),
    }
    r_in = {
        "I": (RI_w_words, RI_w_scales, RI_b),
        "F": (RF_w_words, RF_w_scales, RF_b),
        "O": (RO_w_words, RO_w_scales, RO_b),
        "Z": (RZ_w_words, RZ_w_scales, RZ_b),
    }
    plane_start = {gate: LIVE * i for i, gate in enumerate(GATE_ORDER)}
    bias_cols = {gate: slice(DFF * i, DFF * (i + 1)) for i, gate in enumerate(GATE_ORDER)}

    def live_rows(gate, quad):
        return slice(32 * quad + plane_start[gate], 32 * quad + plane_start[gate] + LIVE)

    with ExitStack() as ctx:
        keep = ctx.enter_context(tc.tile_pool(name="keep", bufs=1))
        acc_pool = ctx.enter_context(tc.psum_pool(name="acc", bufs=1))
        spare = ctx.enter_context(tc.psum_pool(name="spare", bufs=4))

        r_planes = keep.tile([P, Z_GROUPS, DFF], U8, align_bytes=64)
        w_planes = {gate: keep.tile([P, DFF], U8, name="w_planes_%s" % gate, align_bytes=64) for gate in GATE_ORDER}
        bias_rows = keep.tile([P, 4 * DFF + P], BF16)
        ones = keep.tile([P, P], BF16)
        ident = keep.tile([P, P], F32)
        nc.vector.memset(r_planes[:].bitcast(I32), 0)
        for gate in GATE_ORDER:
            nc.vector.memset(w_planes[gate][:].bitcast(I32), 0)
        nc.vector.memset(bias_rows[:], 0.0)
        nc.vector.memset(ones[:], 1.0)
        make_identity(nc, ident[:])

        r_words = {
            gate: [
                keep.tile([P, n, PACK * DFF], U8, name="r_words_%s%d" % (gate, c), align_bytes=64)
                for c, n in enumerate(LOAD_GROUPS[gate])
            ]
            for gate in GATE_ORDER
        }
        w_words = {
            gate: keep.tile([P, PACK * DFF], U8, name="w_words_%s" % gate, align_bytes=64) for gate in GATE_ORDER
        }
        hi_sb = keep.tile([P, DFF], BF16)
        ci_sb = keep.tile([P, DFF], BF16)
        mi_sb = keep.tile([P, DFF], BF16)
        ni_sb = keep.tile([P, DFF], BF16)
        x_codes = keep.tile([P, Z_GROUPS + 1, P], U32, align_bytes=64)
        x_scales = keep.tile([P, Z_GROUPS + 1, P], U8, align_bytes=64)

        def w_scale_loads(gate):
            return [
                (
                    w_planes[gate][live_rows(gate, quad), :].bitcast(I32),
                    w_in[gate][1][0, LIVE * quad : LIVE * (quad + 1), :].bitcast(I32),
                )
                for quad in range(QUADRANTS)
            ]

        with tc.tile_pool(name="x_rows", bufs=1) as x_rows, tc.tile_pool(name="stage", bufs=2) as stage:
            zi_rows = Zi.flatten_outer_dims()
            zi_cols = D // ZI_LOADS
            zi_sb = [x_rows.tile([P, zi_cols], BF16, name="zi_sb%d" % c) for c in range(ZI_LOADS)]
            big_loads = []
            for gate in GATE_ORDER:
                by_partition = r_in[gate][0].rearrange("g p n t -> p g (n t)")
                first_group = 0
                for chunk, n in zip(r_words[gate], LOAD_GROUPS[gate]):
                    big_loads.append(
                        (
                            chunk[:].bitcast(I32),
                            by_partition[:, first_group : first_group + n, :].bitcast(I32),
                            SMALL_PER_BIG if n == LOAD_GROUPS[GATE_ORDER[0]][0] else 0,
                        )
                    )
                    first_group += n
                    if first_group == n:
                        big_loads.append(
                            (
                                w_words[gate][:].bitcast(I32),
                                w_in[gate][0][0].rearrange("p n t -> p (n t)").bitcast(I32),
                                0,
                            )
                        )

            row_inputs = {
                "I": [(hi_sb, Hi)], "F": [(mi_sb, Mi), (ci_sb, Ci), (ni_sb, Ni)], "Z": [], "O": []
            }
            m_cols = slice(4 * DFF, 4 * DFF + P)
            small_loads = []
            for gate in GATE_ORDER:
                small_loads.extend((dst[:], src.flatten_outer_dims()) for dst, src in row_inputs[gate])
                small_loads.extend(w_scale_loads(gate))
                small_loads.append((bias_rows[0:1, bias_cols[gate]], w_in[gate][2].unsqueeze(0)))
                small_loads.append((bias_rows[1:2, bias_cols[gate]], r_in[gate][2].unsqueeze(0)))
                if gate == "I":
                    small_loads.append((bias_rows[0:1, m_cols], m.rearrange("b p one -> one (b p)")))
            waiting = list(reversed(small_loads))

            with tc.manual_schedule(engines={mybir.EngineType.SP, mybir.EngineType.Activation}):
                nc.sync.dma_start(out=zi_sb[0][:], in_=zi_rows[:, :zi_cols])
                for r in range(LIVE):
                    for i, gate in enumerate(GATE_ORDER):
                        dst = r_planes[plane_start[gate] + r : P : 32, :, :]
                        src = r_in[gate][1][:, r : 4 * QUADRANTS : LIVE, :].rearrange("g q n -> q g n")
                        if i % 2 == 0:
                            nc.sync.dma_start(out=dst.bitcast(I32), in_=src.bitcast(I32))
                        else:
                            nc.scalar.dma_start(out=dst.bitcast(F32), in_=src.bitcast(F32))
                big_loads.insert(0, (zi_sb[1][:], zi_rows[:, zi_cols:], 1 + QUADRANTS))
                for dst, src, n in big_loads:
                    nc.sync.dma_start(out=dst, in_=src)
                    for i in range(min(n, len(waiting))):
                        small_dst, small_src = waiting.pop()
                        nc.sync.dma_start(out=small_dst, in_=small_src)

            def quantise(x_sb, n_groups, first_group):
                words = x_sb.bitcast(F32)
                grouped = stage.tile([P, n_groups * K_PASS], BF16, tag="grouped", align_bytes=64)
                grouped_words = grouped[:].bitcast(F32).rearrange("p (g r u) -> p g r u", g=n_groups, u=PAIR)
                in_bank = min(2, n_groups)
                for b in range(n_groups // in_bank):
                    bank = spare.tile([P, in_bank, PAIR, P], F32, tag="spare")
                    for j in range(in_bank):
                        g = in_bank * b + j
                        for u in range(PAIR):
                            nc.tensor.transpose(
                                bank[:, j, u, :], words[:, 256 * g + u : 256 * (g + 1) : PAIR], ident[:]
                            )
                    dst = grouped_words[:, in_bank * b : in_bank * (b + 1)]
                    src = bank[:].rearrange("p g u r -> p g r u")
                    if b % 2 == 0:
                        nc.vector.tensor_copy(out=dst, in_=src)
                    else:
                        nc.scalar.copy(out=dst, in_=src)
                groups = slice(first_group, first_group + n_groups)
                nc.vector.quantize_mx(
                    out=x_codes[:, groups, :].rearrange("p g r -> p (g r)").bitcast(FP8X4),
                    scales=x_scales[:, groups, :].rearrange("p g r -> p (g r)"),
                    in_=grouped[:],
                )

            for c in range(N_CHUNKS):
                load, part = divmod(c, N_CHUNKS // ZI_LOADS)
                quantise(zi_sb[load][:, CHUNK * K_PASS * part : CHUNK * K_PASS * (part + 1)], CHUNK, CHUNK * c)
            quantise(hi_sb[:], 1, HI_GROUP)

        work = ctx.enter_context(tc.tile_pool(name="work", bufs=1))

        def f32_tile(name):
            return work.tile([P, DFF], F32, name=name)

        def gate_products(gate):
            acc = acc_pool.tile([P, DFF], F32, name="acc_%s" % gate)
            first = plane_start[gate]
            slots = [(chunk, j) for chunk, n in zip(r_words[gate], LOAD_GROUPS[gate]) for j in range(n)]
            for g, (chunk, j) in enumerate(slots):
                nc.tensor.matmul_mx(
                    out=acc[:],
                    lhsT=x_codes[:, g, :].bitcast(FP8X4),
                    lhsT_scale=x_scales[:, g, :],
                    rhs=chunk[:, j, :].bitcast(FP8X4),
                    rhs_scale=r_planes[first:P, g, :],
                    start=(g == 0),
                    stop=(g == Z_GROUPS - 1),
                )
                if g == LOAD_GROUPS[gate][0] - 1:
                    nc.tensor.matmul_mx(
                        out=acc[:],
                        lhsT=x_codes[:, HI_GROUP, :].bitcast(FP8X4),
                        lhsT_scale=x_scales[:, HI_GROUP, :],
                        rhs=w_words[gate][:].bitcast(FP8X4),
                        rhs_scale=w_planes[gate][first:P, :],
                        start=False,
                        stop=False,
                    )
            return acc

        acc_i = gate_products("I")

        pre = {}

        def add_biases(gate):
            bias_bank = spare.tile([P, DFF], F32, tag="spare")
            nc.tensor.matmul(out=bias_bank[:], lhsT=ones[:], rhs=bias_rows[:, bias_cols[gate]], start=True, stop=True)
            pre[gate] = f32_tile("pre_%s" % gate)
            if gate == "F":
                nc.vector.tensor_add(out=pre[gate][:], in0=bias_bank[:], in1=mi_sb[:])
            else:
                nc.scalar.copy(out=pre[gate][:], in_=bias_bank[:])
        add_biases("I")
        add_biases("F")
        m_bank = spare.tile([P, DFF], F32, tag="spare")
        nc.tensor.matmul(out=m_bank[:, :32], lhsT=bias_rows[:, m_cols], rhs=ones[:, :32], start=True, stop=True)
        m_f32 = work.tile([P, 1], F32)
        nc.vector.tensor_copy(out=m_f32[:], in_=m_bank[:, 0:1])
        one_minus_m = work.tile([P, 1], F32)
        nc.vector.tensor_scalar(out=one_minus_m[:], in0=m_f32[:], scalar1=-1.0, scalar2=1.0, op0=ALU.mult, op1=ALU.add)
        half_m = work.tile([P, 1], F32)
        nc.vector.tensor_scalar_mul(out=half_m[:], in0=m_f32[:], scalar1=0.5)
        ci_m = f32_tile("ci_m")
        nc.vector.tensor_scalar_mul(out=ci_m[:], in0=ci_sb[:], scalar1=m_f32[:, 0:1])
        ci_keep = f32_tile("ci_keep")
        nc.vector.tensor_scalar_mul(out=ci_keep[:], in0=ci_sb[:], scalar1=one_minus_m[:, 0:1])
        h_rest = f32_tile("h_rest")
        nc.vector.tensor_scalar_mul(out=h_rest[:], in0=hi_sb[:], scalar1=one_minus_m[:, 0:1])

        acc_f = gate_products("F")

        nc.vector.tensor_add(out=pre["I"][:], in0=acc_i[:], in1=pre["I"][:])
        nc.vector.tensor_add(out=pre["F"][:], in0=acc_f[:], in1=pre["F"][:])
        m_t = f32_tile("m_t")
        nc.vector.tensor_max(out=m_t[:], in0=pre["F"][:], in1=pre["I"][:])
        nc.sync.dma_start(out=out_1.flatten_outer_dims(), in_=m_t[:])
        i_t = f32_tile("i_t")
        nc.vector.tensor_sub(out=i_t[:], in0=pre["I"][:], in1=m_t[:])
        nc.scalar.activation(out=i_t[:], in_=i_t[:], func=ACT.Exp)
        f_t = f32_tile("f_t")
        nc.vector.tensor_sub(out=f_t[:], in0=pre["F"][:], in1=m_t[:])
        nc.scalar.activation(out=f_t[:], in_=f_t[:], func=ACT.Exp)
        n_t = f32_tile("n_t")
        nc.vector.tensor_mul(out=n_t[:], in0=f_t[:], in1=ni_sb[:])
        nc.vector.tensor_add(out=n_t[:], in0=n_t[:], in1=i_t[:])
        nc.sync.dma_start(out=out_3.flatten_outer_dims(), in_=n_t[:])
        one_over_n = f32_tile("one_over_n")
        nc.vector.reciprocal(out=one_over_n[:], in_=n_t[:])
        c_t = f32_tile("c_t")
        nc.vector.tensor_mul(out=c_t[:], in0=f_t[:], in1=ci_m[:])
        nc.vector.tensor_add(out=c_t[:], in0=c_t[:], in1=ci_keep[:])

        add_biases("Z")
        add_biases("O")
        acc_z = gate_products("Z")

        nc.vector.tensor_add(out=pre["Z"][:], in0=acc_z[:], in1=pre["Z"][:])
        nc.scalar.activation(out=pre["Z"][:], in_=pre["Z"][:], func=ACT.Tanh)
        nc.vector.tensor_mul(out=pre["Z"][:], in0=pre["Z"][:], in1=i_t[:])
        nc.vector.scalar_tensor_tensor(
            out=c_t[:], in0=pre["Z"][:], scalar=m_f32[:, 0:1], in1=c_t[:], op0=ALU.mult, op1=ALU.add
        )
        nc.sync.dma_start(out=out_0.flatten_outer_dims(), in_=c_t[:])
        h_gain = f32_tile("h_gain")
        nc.vector.scalar_tensor_tensor(
            out=h_gain[:], in0=c_t[:], scalar=half_m[:, 0:1], in1=one_over_n[:], op0=ALU.mult, op1=ALU.mult
        )
        nc.vector.tensor_add(out=h_rest[:], in0=h_rest[:], in1=h_gain[:])

        acc_o = gate_products("O")

        halves = [slice(0, HALF), slice(HALF, DFF)]
        h_t = [f32_tile("h_t%d" % i) for i in range(2)]
        for out, cols in zip(h_t, halves):
            nc.vector.tensor_add(out=out[:, :HALF], in0=acc_o[:, cols], in1=pre["O"][:, cols])
        for out in h_t:
            nc.scalar.activation(out=out[:, :HALF], in_=out[:, :HALF], func=ACT.Tanh, scale=0.5)
        for out, cols in zip(h_t, halves):
            nc.vector.tensor_mul(out=out[:, :HALF], in0=out[:, :HALF], in1=h_gain[:, cols])
        for out, cols in zip(h_t, halves):
            nc.vector.tensor_add(out=out[:, :HALF], in0=out[:, :HALF], in1=h_rest[:, cols])
            nc.sync.dma_start(out=out_2.flatten_outer_dims()[:, cols], in_=out[:, :HALF])
